import numpy as np
import ml_dtypes


def mxq(x, axis, fmt="e4m3"):
    dtype, down = {"e4m3": (ml_dtypes.float8_e4m3fn, 7), "e5m2": (ml_dtypes.float8_e5m2, 14)}[fmt]
    v = np.moveaxis(np.asarray(x, np.float32).astype(ml_dtypes.bfloat16).astype(np.float64), axis, -1)
    blocks = v.reshape(v.shape[:-1] + (-1, 32))
    amax = np.abs(blocks).max(-1, keepdims=True)
    byte = np.maximum(np.where(amax > 0, np.frexp(amax)[1] - 1 + 127, 0) - down, 1)
    scale = np.exp2(byte - 127.0)
    codes = (blocks / scale).astype(np.float32).astype(dtype).astype(np.float64)
    return np.moveaxis((codes * scale).reshape(v.shape), -1, axis)


WIDE = False


def mx_kscale(k):
    if not WIDE:
        return np.ones(k)
    levels = np.array([10, -10, 5, -5, 0])
    if k % 512:
        return np.exp2(np.random.permutation(np.resize(levels, k // 32))).repeat(32)
    a = np.empty((k // 512, 16))
    for p in range(k // 512):
        a[p, :8] = np.random.permutation(np.resize(levels, 8))
        for g in range(8):
            far = levels[np.abs(levels - a[p, g]) >= 10]
            a[p, g + 8] = far[np.random.randint(len(far))]
    return np.exp2(a.ravel()).repeat(32)


BF16 = ml_dtypes.bfloat16


def bf(x):
    return np.asarray(x, np.float32).astype(BF16)


def f64(x):
    return np.asarray(x).astype(np.float64)


B, T, D, C, M = 4, 2048, 1024, 128, 4
NB = T // M
NEG = -1e30


def setup_inputs():
    s = mx_kscale(D)
    w = 1.0 / np.sqrt(D)
    return {
        "H": bf(np.random.standard_normal((B, T, D)) * s),
        "W_a_KV": bf(np.random.standard_normal((D, C)) * w / s[:, None]),
        "W_b_KV": bf(np.random.standard_normal((D, C)) * w / s[:, None]),
        "W_a_Z": bf(np.random.standard_normal((D, C)) * w / s[:, None]),
        "W_b_Z": bf(np.random.standard_normal((D, C)) * w / s[:, None]),
        "B_a": bf(np.random.standard_normal((M, C))),
        "B_b": bf(np.random.standard_normal((M, C))),
    }


def reference(H, W_a_KV, W_b_KV, W_a_Z, W_b_Z, B_a, B_b):
    Hq = mxq(f64(H), 2, "e4m3")
    C_a = (Hq @ mxq(f64(W_a_KV), 0, "e4m3")).reshape(B, NB, M, C)
    C_b = (Hq @ mxq(f64(W_b_KV), 0, "e4m3")).reshape(B, NB, M, C)
    Z_a = (Hq @ mxq(f64(W_a_Z), 0, "e4m3")).reshape(B, NB, M, C) + f64(B_a)
    Z_b = (Hq @ mxq(f64(W_b_Z), 0, "e4m3")).reshape(B, NB, M, C) + f64(B_b)
    Z_b_prev = np.concatenate([np.full((B, 1, M, C), NEG), Z_b[:, :-1]], axis=1)
    C_b_prev = np.concatenate([np.zeros((B, 1, M, C)), C_b[:, :-1]], axis=1)
    logits = np.concatenate([Z_a, Z_b_prev], axis=2)
    vals = np.concatenate([C_a, C_b_prev], axis=2)
    e = np.exp(logits - logits.max(axis=2, keepdims=True))
    probs = e / e.sum(axis=2, keepdims=True)
    return (probs * vals).sum(axis=2)

@@ -1,0 +1,306 @@
+from contextlib import ExitStack
+
+import concourse.mybir as mybir
+from concourse.masks import make_identity
+
+F32 = mybir.dt.float32
+BF16 = mybir.dt.bfloat16
+U32 = mybir.dt.uint32
+U8 = mybir.dt.uint8
+FP8X4 = mybir.dt.float8_e4m3fn_x4
+ALU = mybir.AluOpType
+ACT = mybir.ActivationFunctionType
+
+P = 128
+BATCHES = 4
+FEATURES = 1024
+CHANNELS = 128
+POSITIONS = 4
+GROUPS = 4
+ROWS = 128
+PASSES = 2
+HALVES = 2
+VALUES = 4
+TOKENS = POSITIONS * ROWS
+WORDS = FEATURES // 2
+TERMS = 2 * POSITIONS
+NEG = -1e30
+W_KV_A, W_KV_B, W_Z_A, W_Z_B = 0, 1, 2, 3
+STEPS = BATCHES * GROUPS
+QUANTISE_AHEAD = 3
+TURN_AHEAD = 4
+FETCH_AHEAD = 6
+BANKS = PASSES * POSITIONS // 2
+
+FLOPS = 2 * BATCHES * GROUPS * TOKENS * FEATURES * 4 * CHANNELS
+
+
+def tile_tokencompressor_pa_t_kernel(tc, H, W_a_KV, W_b_KV, W_a_Z, W_b_Z, B_a, B_b, out):
+    nc = tc.nc
+    with ExitStack() as ctx:
+        ctx.enter_context(tc.manual_schedule())
+        const = ctx.enter_context(tc.tile_pool(name="const", bufs=1))
+        raw_pool = ctx.enter_context(tc.tile_pool(name="raw", bufs=FETCH_AHEAD))
+        grouped_pool = ctx.enter_context(tc.tile_pool(name="grouped", bufs=3))
+        code_pool = ctx.enter_context(tc.tile_pool(name="codes", bufs=8))
+        soft_pool = ctx.enter_context(tc.tile_pool(name="soft", bufs=3))
+        out_pool = ctx.enter_context(tc.tile_pool(name="outs", bufs=2))
+        psum_t = ctx.enter_context(tc.psum_pool(name="psum_t", bufs=3))
+        psum_mx = ctx.enter_context(tc.psum_pool(name="psum_mx", bufs=1))
+        psum_sum = ctx.enter_context(tc.psum_pool(name="psum_sum", bufs=1))
+
+        arrival = [(n, q) for n in range(BATCHES) for q in (3, 0, 1, 2)]
+        steps = [(n, q) for n in range(BATCHES) for q in range(GROUPS)]
+        raw_of = {}
+        grouped_of = {}
+        quantised = {}
+        banks = {}
+        weights_of = {}
+        values_b_of = {}
+        halved_of = {}
+
+        def fetch(i):
+            n, q = arrival[i]
+            raw = raw_pool.tile([P, POSITIONS, FEATURES], BF16)
+            nc.sync.dma_start(
+                out=raw[:].rearrange("r j k -> r (j k)"),
+                in_=H[n].rearrange("(r q j) k -> q r (j k)", q=GROUPS, j=POSITIONS)[q],
+            )
+            raw_of[i] = raw
+
+        fetch(0)
+        w_raw = const.tile([P, 4, PASSES, VALUES * CHANNELS], BF16)
+        for w, weight in enumerate((W_a_KV, W_b_KV, W_a_Z, W_b_Z)):
+            nc.sync.dma_start(
+                out=w_raw[:, w, :, :], in_=weight.rearrange("(g p t) c -> p g (t c)", g=PASSES, t=VALUES)
+            )
+        for i in range(1, FETCH_AHEAD):
+            fetch(i)
+
+        ident = const.tile([P, P], F32)
+        make_identity(nc, ident[:])
+
+        bias_rows = const.tile([P, CHANNELS], BF16)
+        nc.vector.memset(bias_rows[:], 0.0)
+        nc.scalar.dma_start(out=bias_rows[0:POSITIONS, :], in_=B_a)
+        nc.scalar.dma_start(out=bias_rows[POSITIONS:TERMS, :], in_=B_b)
+        bias_rows32 = const.tile([P, CHANNELS], F32)
+        nc.vector.tensor_copy(out=bias_rows32[:], in_=bias_rows[:])
+
+        w_grouped = const.tile([P, 4 * PASSES, CHANNELS, 4], BF16, align_bytes=64)
+        nc.vector.tensor_copy(
+            out=w_grouped[:],
+            in_=w_raw[:].rearrange("p w g (t c) -> p (w g) c t", t=VALUES),
+        )
+        w_codes = const.tile([P, 4 * PASSES, CHANNELS], U32, align_bytes=64)
+        w_scales = const.tile([P, 4 * PASSES, CHANNELS], U8, align_bytes=64)
+        nc.vector.quantize_mx(
+            out=w_codes[:].rearrange("p a c -> p (a c)").bitcast(FP8X4),
+            scales=w_scales[:].rearrange("p a c -> p (a c)"),
+            in_=w_grouped[:].rearrange("p a c t -> p (a c t)"),
+        )
+
+        totals = const.tile([P, STEPS, 2, CHANNELS], F32)
+
+        def turn(i, some_banks):
+            raw_words = raw_of[i][:].bitcast(F32)
+            if i not in grouped_of:
+                grouped = grouped_pool.tile([P, PASSES, 4 * TOKENS], BF16, align_bytes=64)
+                grouped_of[i] = grouped
+            for bank in some_banks:
+                g, pair = divmod(bank, POSITIONS // 2)
+                turned = psum_t.tile([P, HALVES, 2, ROWS], F32)
+                for u in range(HALVES):
+                    for jj in range(2):
+                        nc.tensor.transpose(
+                            turned[:, u, jj, :],
+                            raw_words[:, 2 * pair + jj, 2 * P * g + u : 2 * P * (g + 1) : HALVES],
+                            ident[:],
+                        )
+                columns = grouped_of[i][:, g, 8 * ROWS * pair : 8 * ROWS * (pair + 1)].bitcast(F32)
+                nc.scalar.copy(
+                    out=columns.rearrange("p (c u) -> p c u", u=HALVES),
+                    in_=turned[:].rearrange("p u j r -> p (j r) u"),
+                )
+
+        def quantise(i):
+            codes = code_pool.tile([P, PASSES, TOKENS], U32, align_bytes=64)
+            scales = code_pool.tile([P, PASSES, TOKENS], U8, align_bytes=64)
+            nc.vector.quantize_mx(
+                out=codes[:].rearrange("p g c -> p (g c)").bitcast(FP8X4),
+                scales=scales[:].rearrange("p g c -> p (g c)"),
+                in_=grouped_of[i][:].rearrange("p g c -> p (g c)"),
+            )
+            quantised[arrival[i]] = (codes, scales)
+
+        def project(name, w, operand, s):
+            codes, scales = operand
+            bank = psum_mx.tile([P, POSITIONS, ROWS], F32, tag=name)
+            for g in range(PASSES):
+                nc.tensor.matmul_mx(
+                    out=bank[:].rearrange("p j r -> p (j r)"),
+                    lhsT=w_codes[:, PASSES * w + g, :].bitcast(FP8X4),
+                    lhsT_scale=w_scales[:, PASSES * w + g, :],
+                    rhs=codes[:, g, :].bitcast(FP8X4),
+                    rhs_scale=scales[:, g, :],
+                    start=(g == 0),
+                    stop=(g == PASSES - 1),
+                )
+            banks[(name, s)] = bank
+
+        def own_and_previous(s):
+            n, q = steps[s]
+            return quantised[(n, q)], quantised[(n, (q - 1) % GROUPS)]
+
+        def logits(s):
+            own, previous = own_and_previous(s)
+            project("z_a", W_Z_A, own, s)
+            project("z_b", W_Z_B, previous, s)
+
+        def values(s):
+            own, previous = own_and_previous(s)
+            project("c_a", W_KV_A, own, s)
+            project("c_b", W_KV_B, previous, s)
+            values_b = soft_pool.tile([P, POSITIONS, ROWS], F32)
+            nc.scalar.copy(out=values_b[:], in_=banks[("c_b", s)][:])
+            values_b_of[s] = values_b
+
+        def shift_of(s):
+            return 1 if steps[s][1] == 0 else 0
+
+        def halve(name, s, terms):
+            halved = soft_pool.tile([P, POSITIONS, ROWS], F32, tag=name + "_halved")
+            nc.gpsimd.tensor_tensor(
+                out=halved[:], in0=terms[:, 0:POSITIONS, :], in1=terms[:, POSITIONS:TERMS, :], op=ALU.add
+            )
+            halved_of[(name, s)] = halved
+
+        def soften(s):
+            shift = shift_of(s)
+            kept = ROWS - shift
+            z_a = banks[("z_a", s)]
+            z_b = banks[("z_b", s)]
+            top_a = soft_pool.tile([P, ROWS], F32)
+            top_b = soft_pool.tile([P, ROWS], F32)
+            nc.vector.tensor_scalar_add(out=top_a[:], in0=z_a[:, 0, :], scalar1=bias[:, 0:1])
+            nc.vector.tensor_scalar_add(
+                out=top_b[:, shift:], in0=z_b[:, 0, 0:kept], scalar1=bias[:, POSITIONS : POSITIONS + 1]
+            )
+            for j in range(1, POSITIONS):
+                nc.vector.scalar_tensor_tensor(
+                    out=top_a[:], in0=z_a[:, j, :], scalar=bias[:, j : j + 1], in1=top_a[:], op0=ALU.add, op1=ALU.max
+                )
+                nc.vector.scalar_tensor_tensor(
+                    out=top_b[:, shift:],
+                    in0=z_b[:, j, 0:kept],
+                    scalar=bias[:, POSITIONS + j : POSITIONS + j + 1],
+                    in1=top_b[:, shift:],
+                    op0=ALU.add,
+                    op1=ALU.max,
+                )
+            nc.vector.tensor_tensor(out=top_a[:, shift:], in0=top_a[:, shift:], in1=top_b[:, shift:], op=ALU.max)
+
+            weights = soft_pool.tile([P, TERMS, ROWS], F32)
+            for j in range(POSITIONS):
+                nc.vector.scalar_tensor_tensor(
+                    out=weights[:, j, :],
+                    in0=z_a[:, j, :],
+                    scalar=bias[:, j : j + 1],
+                    in1=top_a[:],
+                    op0=ALU.add,
+                    op1=ALU.subtract,
+                )
+            nc.scalar.activation(out=weights[:, 0:POSITIONS, :], in_=weights[:, 0:POSITIONS, :], func=ACT.Exp)
+            if shift:
+                nc.vector.memset(weights[:, POSITIONS:TERMS, 0:shift], NEG)
+            for j in range(POSITIONS):
+                nc.vector.scalar_tensor_tensor(
+                    out=weights[:, POSITIONS + j, shift:],
+                    in0=z_b[:, j, 0:kept],
+                    scalar=bias[:, POSITIONS + j : POSITIONS + j + 1],
+                    in1=top_a[:, shift:],
+                    op0=ALU.add,
+                    op1=ALU.subtract,
+                )
+            nc.scalar.activation(out=weights[:, POSITIONS:TERMS, :], in_=weights[:, POSITIONS:TERMS, :], func=ACT.Exp)
+            weights_of[s] = weights
+            halve("weights", s, weights)
+
+        def weigh(s):
+            shift = shift_of(s)
+            kept = ROWS - shift
+            weights = weights_of[s]
+            weighted = soft_pool.tile([P, TERMS, ROWS], F32)
+            nc.vector.tensor_tensor(
+                out=weighted[:, 0:POSITIONS, :], in0=banks[("c_a", s)][:], in1=weights[:, 0:POSITIONS, :], op=ALU.mult
+            )
+            if shift:
+                nc.gpsimd.memset(weighted[:, POSITIONS:TERMS, 0:shift], 0.0)
+            nc.gpsimd.tensor_tensor(
+                out=weighted[:, POSITIONS:TERMS, shift:],
+                in0=values_b_of[s][:, :, 0:kept],
+                in1=weights[:, POSITIONS:TERMS, shift:],
+                op=ALU.mult,
+            )
+            halve("weighted", s, weighted)
+
+        def total(s):
+            sums = psum_sum.tile([P, 2, CHANNELS], F32, tag="sums")
+            for place, name in enumerate(("weights", "weighted")):
+                for j in range(POSITIONS):
+                    nc.tensor.matmul(
+                        out=sums[:, place, :],
+                        lhsT=halved_of[(name, s)][:, j, :],
+                        rhs=ident[:],
+                        is_transpose=True,
+                        start=(j == 0),
+                        stop=(j == POSITIONS - 1),
+                    )
+            nc.scalar.copy(out=totals[:, s, :, :], in_=sums[:])
+
+        def divide_and_store(n):
+            mine = slice(GROUPS * n, GROUPS * (n + 1))
+            inverse = out_pool.tile([P, GROUPS, CHANNELS], F32)
+            nc.scalar.activation(out=inverse[:], in_=totals[:, mine, 0, :], func=ACT.Abs_reciprocal_sqrt)
+            nc.scalar.activation(out=inverse[:], in_=inverse[:], func=ACT.Square)
+            result = out_pool.tile([P, GROUPS, CHANNELS], F32)
+            nc.vector.tensor_tensor(out=result[:], in0=totals[:, mine, 1, :], in1=inverse[:], op=ALU.mult)
+            nc.sync.dma_start(
+                out=out[n].rearrange("(r q) c -> r (q c)", q=GROUPS), in_=result[:].rearrange("r q c -> r (q c)")
+            )
+
+        every_bank = range(BANKS)
+        turn(0, every_bank)
+        bias_t = psum_sum.tile([P, 2, P], F32, tag="sums")
+        nc.tensor.transpose(bias_t[:, 0, :], bias_rows32[:], ident[:])
+        bias = const.tile([P, TERMS], F32)
+        nc.vector.tensor_copy(out=bias[:], in_=bias_t[:, 0, 0:TERMS])
+        for i in range(1, QUANTISE_AHEAD):
+            turn(i, every_bank)
+        for i in range(QUANTISE_AHEAD):
+            quantise(i)
+        logits(0)
+        values(0)
+        for i in range(QUANTISE_AHEAD, TURN_AHEAD):
+            turn(i, every_bank)
+        for s in range(STEPS):
+            soften(s)
+            if s + QUANTISE_AHEAD < STEPS:
+                quantise(s + QUANTISE_AHEAD)
+            if s + 1 < STEPS:
+                logits(s + 1)
+            weigh(s)
+            if s + FETCH_AHEAD < STEPS:
+                fetch(s + FETCH_AHEAD)
+            if s + TURN_AHEAD < STEPS:
+                turn(s + TURN_AHEAD, every_bank[: BANKS - 1])
+            if s > 0:
+                total(s - 1)
+            if s + TURN_AHEAD < STEPS:
+                turn(s + TURN_AHEAD, every_bank[BANKS - 1 :])
+            if s + 1 < STEPS:
+                values(s + 1)
+        for n in range(BATCHES - 1):
+            divide_and_store(n)
+        total(STEPS - 1)
+        divide_and_store(BATCHES - 1)

@@ -30,6 +30,9 @@ STEPS = BATCHES * GROUPS
 QUANTISE_AHEAD = 3
 TURN_AHEAD = 4
 FETCH_AHEAD = 6
+HEAD = 2
+PAIRS = 2
+LATE = STEPS - TURN_AHEAD
 BANKS = PASSES * POSITIONS // 2
 
 FLOPS = 2 * BATCHES * GROUPS * TOKENS * FEATURES * 4 * CHANNELS
@@ -57,59 +60,73 @@ def tile_tokencompressor_pa_t_kernel(tc, H, W_a_KV, W_b_KV, W_a_Z, W_b_Z, B_a, B
         banks = {}
         weights_of = {}
         values_b_of = {}
+        sums_of = {}
         halved_of = {}
 
-        def fetch(i):
+        def fetch(i, pieces=1):
             n, q = arrival[i]
             raw = raw_pool.tile([P, POSITIONS, FEATURES], BF16)
-            nc.sync.dma_start(
-                out=raw[:].rearrange("r j k -> r (j k)"),
-                in_=H[n].rearrange("(r q j) k -> q r (j k)", q=GROUPS, j=POSITIONS)[q],
-            )
+            rows = H[n].rearrange("(r q j) k -> q r j k", q=GROUPS, j=POSITIONS)[q]
+            for piece in range(pieces):
+                mine = slice(piece * POSITIONS // pieces, (piece + 1) * POSITIONS // pieces)
+                nc.sync.dma_start(out=raw[:, mine, :], in_=rows[:, mine, :])
             raw_of[i] = raw
 
-        fetch(0)
         w_raw = const.tile([P, 4, PASSES, VALUES * CHANNELS], BF16)
-        for w, weight in enumerate((W_a_KV, W_b_KV, W_a_Z, W_b_Z)):
-            nc.sync.dma_start(
-                out=w_raw[:, w, :, :], in_=weight.rearrange("(g p t) c -> p g (t c)", g=PASSES, t=VALUES)
-            )
-        for i in range(1, FETCH_AHEAD):
+        weights_in = (W_a_KV, W_b_KV, W_a_Z, W_b_Z)
+
+        def fetch_weights(places):
+            for w in places:
+                nc.sync.dma_start(
+                    out=w_raw[:, w, :, :], in_=weights_in[w].rearrange("(g p t) c -> p g (t c)", g=PASSES, t=VALUES)
+                )
+
+        bias_rows = const.tile([P, CHANNELS], BF16)
+        nc.vector.memset(bias_rows[:], 0.0)
+        fetch_weights((W_Z_A, W_Z_B))
+        nc.sync.dma_start(out=bias_rows[0:POSITIONS, :], in_=B_a)
+        nc.sync.dma_start(out=bias_rows[POSITIONS:TERMS, :], in_=B_b)
+        fetch(0, PAIRS)
+        fetch_weights((W_KV_A, W_KV_B))
+        fetch(1, PAIRS)
+        for i in range(HEAD, FETCH_AHEAD):
             fetch(i)
 
         ident = const.tile([P, P], F32)
         make_identity(nc, ident[:])
 
-        bias_rows = const.tile([P, CHANNELS], BF16)
-        nc.vector.memset(bias_rows[:], 0.0)
-        nc.scalar.dma_start(out=bias_rows[0:POSITIONS, :], in_=B_a)
-        nc.scalar.dma_start(out=bias_rows[POSITIONS:TERMS, :], in_=B_b)
         bias_rows32 = const.tile([P, CHANNELS], F32)
-        nc.vector.tensor_copy(out=bias_rows32[:], in_=bias_rows[:])
+        nc.gpsimd.tensor_copy(out=bias_rows32[:], in_=bias_rows[:])
 
-        w_grouped = const.tile([P, 4 * PASSES, CHANNELS, 4], BF16, align_bytes=64)
-        nc.vector.tensor_copy(
-            out=w_grouped[:],
-            in_=w_raw[:].rearrange("p w g (t c) -> p (w g) c t", t=VALUES),
-        )
+        w_grouped = const.tile([P, 4 * PASSES, CHANNELS, VALUES], BF16, align_bytes=64)
         w_codes = const.tile([P, 4 * PASSES, CHANNELS], U32, align_bytes=64)
         w_scales = const.tile([P, 4 * PASSES, CHANNELS], U8, align_bytes=64)
-        nc.vector.quantize_mx(
-            out=w_codes[:].rearrange("p a c -> p (a c)").bitcast(FP8X4),
-            scales=w_scales[:].rearrange("p a c -> p (a c)"),
-            in_=w_grouped[:].rearrange("p a c t -> p (a c t)"),
-        )
+
+        def group_weights(places):
+            for w in places:
+                nc.vector.tensor_copy(
+                    out=w_grouped[:, PASSES * w : PASSES * (w + 1), :, :],
+                    in_=w_raw[:, w, :, :].rearrange("p g (t c) -> p g c t", t=VALUES),
+                )
+
+        def quantise_weights(places):
+            mine = slice(PASSES * places[0], PASSES * (places[-1] + 1))
+            nc.vector.quantize_mx(
+                out=w_codes[:, mine, :].rearrange("p a c -> p (a c)").bitcast(FP8X4),
+                scales=w_scales[:, mine, :].rearrange("p a c -> p (a c)"),
+                in_=w_grouped[:, mine, :, :].rearrange("p a c t -> p (a c t)"),
+            )
 
         totals = const.tile([P, STEPS, 2, CHANNELS], F32)
 
-        def turn(i, some_banks):
+        def turn(i, some_banks, copies):
             raw_words = raw_of[i][:].bitcast(F32)
             if i not in grouped_of:
                 grouped = grouped_pool.tile([P, PASSES, 4 * TOKENS], BF16, align_bytes=64)
                 grouped_of[i] = grouped
-            for bank in some_banks:
+            for bank, copy in zip(some_banks, copies):
                 g, pair = divmod(bank, POSITIONS // 2)
-                turned = psum_t.tile([P, HALVES, 2, ROWS], F32)
+                turned = psum_t.tile([P, HALVES, 2, ROWS], F32, tag="turned")
                 for u in range(HALVES):
                     for jj in range(2):
                         nc.tensor.transpose(
@@ -118,14 +135,29 @@ def tile_tokencompressor_pa_t_kernel(tc, H, W_a_KV, W_b_KV, W_a_Z, W_b_Z, B_a, B
                             ident[:],
                         )
                 columns = grouped_of[i][:, g, 8 * ROWS * pair : 8 * ROWS * (pair + 1)].bitcast(F32)
-                nc.scalar.copy(
+                copy(
                     out=columns.rearrange("p (c u) -> p c u", u=HALVES),
                     in_=turned[:].rearrange("p u j r -> p (j r) u"),
                 )
 
+        def quantise_pair(i, pair):
+            if arrival[i] not in quantised:
+                codes = code_pool.tile([P, PASSES, TOKENS], U32, tag="codes", align_bytes=64)
+                scales = code_pool.tile([P, PASSES, TOKENS], U8, tag="scales", align_bytes=64)
+                quantised[arrival[i]] = (codes, scales)
+            codes, scales = quantised[arrival[i]]
+            width = TOKENS // PAIRS
+            for g in range(PASSES):
+                mine = slice(width * pair, width * (pair + 1))
+                nc.vector.quantize_mx(
+                    out=codes[:, g, mine].bitcast(FP8X4),
+                    scales=scales[:, g, mine],
+                    in_=grouped_of[i][:, g, VALUES * width * pair : VALUES * width * (pair + 1)],
+                )
+
         def quantise(i):
-            codes = code_pool.tile([P, PASSES, TOKENS], U32, align_bytes=64)
-            scales = code_pool.tile([P, PASSES, TOKENS], U8, align_bytes=64)
+            codes = code_pool.tile([P, PASSES, TOKENS], U32, tag="codes", align_bytes=64)
+            scales = code_pool.tile([P, PASSES, TOKENS], U8, tag="scales", align_bytes=64)
             nc.vector.quantize_mx(
                 out=codes[:].rearrange("p g c -> p (g c)").bitcast(FP8X4),
                 scales=scales[:].rearrange("p g c -> p (g c)"),
@@ -133,19 +165,27 @@ def tile_tokencompressor_pa_t_kernel(tc, H, W_a_KV, W_b_KV, W_a_Z, W_b_Z, B_a, B
             )
             quantised[arrival[i]] = (codes, scales)
 
-        def project(name, w, operand, s):
+        def project(name, w, operand, s, pieces=1):
             codes, scales = operand
-            bank = psum_mx.tile([P, POSITIONS, ROWS], F32, tag=name)
-            for g in range(PASSES):
-                nc.tensor.matmul_mx(
-                    out=bank[:].rearrange("p j r -> p (j r)"),
-                    lhsT=w_codes[:, PASSES * w + g, :].bitcast(FP8X4),
-                    lhsT_scale=w_scales[:, PASSES * w + g, :],
-                    rhs=codes[:, g, :].bitcast(FP8X4),
-                    rhs_scale=scales[:, g, :],
-                    start=(g == 0),
-                    stop=(g == PASSES - 1),
-                )
+            if s > LATE and s % 2 == 1 and name in ("z_a", "z_b"):
+                bank = psum_t.tile([P, POSITIONS, ROWS], F32, tag="turned")
+            else:
+                tag = name.replace("c_", "z_") if s == STEPS - 1 else name
+                bank = psum_mx.tile([P, POSITIONS, ROWS], F32, tag=tag)
+            sums = bank[:].rearrange("p j r -> p (j r)")
+            width = TOKENS // pieces
+            for piece in range(pieces):
+                mine = slice(width * piece, width * (piece + 1))
+                for g in range(PASSES):
+                    nc.tensor.matmul_mx(
+                        out=sums[:, mine],
+                        lhsT=w_codes[:, PASSES * w + g, :].bitcast(FP8X4),
+                        lhsT_scale=w_scales[:, PASSES * w + g, :],
+                        rhs=codes[:, g, mine].bitcast(FP8X4),
+                        rhs_scale=scales[:, g, mine],
+                        start=(g == 0),
+                        stop=(g == PASSES - 1),
+                    )
             banks[(name, s)] = bank
 
         def own_and_previous(s):
@@ -161,14 +201,18 @@ def tile_tokencompressor_pa_t_kernel(tc, H, W_a_KV, W_b_KV, W_a_Z, W_b_Z, B_a, B
             own, previous = own_and_previous(s)
             project("c_a", W_KV_A, own, s)
             project("c_b", W_KV_B, previous, s)
-            values_b = soft_pool.tile([P, POSITIONS, ROWS], F32)
-            nc.scalar.copy(out=values_b[:], in_=banks[("c_b", s)][:])
-            values_b_of[s] = values_b
+            if s < STEPS - 1:
+                values_b = soft_pool.tile([P, POSITIONS, ROWS], F32)
+                nc.scalar.copy(out=values_b[:], in_=banks[("c_b", s)][:])
+                values_b_of[s] = values_b
 
         def shift_of(s):
             return 1 if steps[s][1] == 0 else 0
 
         def halve(name, s, terms):
+            if s >= LATE:
+                halved_of[(name, s)] = terms
+                return
             halved = soft_pool.tile([P, POSITIONS, ROWS], F32, tag=name + "_halved")
             nc.gpsimd.tensor_tensor(
                 out=halved[:], in0=terms[:, 0:POSITIONS, :], in1=terms[:, POSITIONS:TERMS, :], op=ALU.add
@@ -236,71 +280,159 @@ def tile_tokencompressor_pa_t_kernel(tc, H, W_a_KV, W_b_KV, W_a_Z, W_b_Z, B_a, B
             )
             if shift:
                 nc.gpsimd.memset(weighted[:, POSITIONS:TERMS, 0:shift], 0.0)
-            nc.gpsimd.tensor_tensor(
+            engine, values_b = (nc.gpsimd, values_b_of[s]) if s < STEPS - 1 else (nc.vector, banks[("c_b", s)])
+            engine.tensor_tensor(
                 out=weighted[:, POSITIONS:TERMS, shift:],
-                in0=values_b_of[s][:, :, 0:kept],
+                in0=values_b[:, :, 0:kept],
                 in1=weights[:, POSITIONS:TERMS, shift:],
                 op=ALU.mult,
             )
             halve("weighted", s, weighted)
 
         def total(s):
-            sums = psum_sum.tile([P, 2, CHANNELS], F32, tag="sums")
+            if s < STEPS - 2:
+                sums = psum_sum.tile([P, 2, CHANNELS], F32, tag="sums")
+            else:
+                sums = psum_t.tile([P, 2, CHANNELS], F32, tag="turned")
             for place, name in enumerate(("weights", "weighted")):
-                for j in range(POSITIONS):
+                terms = POSITIONS if s < LATE else TERMS
+                for j in range(terms):
                     nc.tensor.matmul(
                         out=sums[:, place, :],
                         lhsT=halved_of[(name, s)][:, j, :],
                         rhs=ident[:],
                         is_transpose=True,
                         start=(j == 0),
-                        stop=(j == POSITIONS - 1),
+                        stop=(j == terms - 1),
                     )
-            nc.scalar.copy(out=totals[:, s, :, :], in_=sums[:])
+            if s < STEPS - 2:
+                nc.scalar.copy(out=totals[:, s, :, :], in_=sums[:])
+            else:
+                sums_of[s] = sums
 
-        def divide_and_store(n):
-            mine = slice(GROUPS * n, GROUPS * (n + 1))
-            inverse = out_pool.tile([P, GROUPS, CHANNELS], F32)
-            nc.scalar.activation(out=inverse[:], in_=totals[:, mine, 0, :], func=ACT.Abs_reciprocal_sqrt)
-            nc.scalar.activation(out=inverse[:], in_=inverse[:], func=ACT.Square)
-            result = out_pool.tile([P, GROUPS, CHANNELS], F32)
-            nc.vector.tensor_tensor(out=result[:], in0=totals[:, mine, 1, :], in1=inverse[:], op=ALU.mult)
-            nc.sync.dma_start(
-                out=out[n].rearrange("(r q) c -> r (q c)", q=GROUPS), in_=result[:].rearrange("r q c -> r (q c)")
+        roots = const.tile([P, STEPS, CHANNELS], F32)
+        results = const.tile([P, STEPS, CHANNELS], F32)
+
+        def steps_of(part):
+            return slice(part[0], part[-1] + 1)
+
+        def both_sums(part, place):
+            if part[0] in sums_of:
+                return sums_of[part[0]][:, place, :]
+            return totals[:, steps_of(part), place, :]
+
+        def root(part):
+            out_ = roots[:, part[0], :] if part[0] in sums_of else roots[:, steps_of(part), :]
+            nc.scalar.activation(out=out_, in_=both_sums(part, 0), func=ACT.Abs_reciprocal_sqrt)
+
+        def square(part):
+            mine = roots[:, steps_of(part), :]
+            nc.scalar.activation(out=mine, in_=mine, func=ACT.Square)
+
+        def times_root(part, first):
+            one = part[0] in sums_of
+            mine = results[:, part[0], :] if one else results[:, steps_of(part), :]
+            nc.vector.tensor_tensor(
+                out=mine,
+                in0=both_sums(part, 1) if first else mine,
+                in1=roots[:, part[0], :] if one else roots[:, steps_of(part), :],
+                op=ALU.mult,
             )
 
+        def store(n):
+            mine = slice(GROUPS * n, GROUPS * (n + 1))
+            nc.sync.dma_start(
+                out=out[n].rearrange("(r q) c -> r (q c)", q=GROUPS), in_=results[:, mine, :].rearrange("r q c -> r (q c)")
+            )
+
+        S_COPY, V_COPY = nc.scalar.copy, nc.vector.tensor_copy
         every_bank = range(BANKS)
-        turn(0, every_bank)
+        pair_banks = [[g * PAIRS + pair for g in range(PASSES)] for pair in range(PAIRS)]
+
+        group_weights((W_Z_A, W_Z_B))
+        quantise_weights((W_Z_A, W_Z_B))
+        turn(0, pair_banks[0], (S_COPY, S_COPY))
+        turn(0, pair_banks[1], (S_COPY, S_COPY))
+        quantise_pair(0, 0)
+        group_weights((W_KV_A, W_KV_B))
+        quantise_pair(0, 1)
+        quantise_weights((W_KV_A, W_KV_B))
+        turn(1, pair_banks[0], (S_COPY, S_COPY))
+        turn(1, pair_banks[1], (S_COPY, V_COPY))
         bias_t = psum_sum.tile([P, 2, P], F32, tag="sums")
         nc.tensor.transpose(bias_t[:, 0, :], bias_rows32[:], ident[:])
         bias = const.tile([P, TERMS], F32)
-        nc.vector.tensor_copy(out=bias[:], in_=bias_t[:, 0, 0:TERMS])
-        for i in range(1, QUANTISE_AHEAD):
-            turn(i, every_bank)
-        for i in range(QUANTISE_AHEAD):
-            quantise(i)
-        logits(0)
+        nc.scalar.copy(out=bias[:], in_=bias_t[:, 0, 0:TERMS])
+        project("z_b", W_Z_B, quantised[arrival[0]], 0)
+        quantise_pair(1, 0)
+        quantise_pair(1, 1)
+        project("z_a", W_Z_A, quantised[arrival[1]], 0, PAIRS)
+        turn(2, every_bank[:3], (S_COPY,) * 3)
+        soften(0)
+        turn(2, every_bank[3:], (V_COPY,))
         values(0)
-        for i in range(QUANTISE_AHEAD, TURN_AHEAD):
-            turn(i, every_bank)
+        turn(3, every_bank[:2], (S_COPY,) * 2)
+        quantise(2)
         for s in range(STEPS):
-            soften(s)
-            if s + QUANTISE_AHEAD < STEPS:
-                quantise(s + QUANTISE_AHEAD)
+            if s >= LATE:
+                if s < STEPS - 1:
+                    total(s - 1)
+                if s + QUANTISE_AHEAD < STEPS:
+                    quantise(s + QUANTISE_AHEAD)
+                if s + 2 < STEPS:
+                    logits(s + 2)
+                if s + 2 == STEPS:
+                    values(s + 1)
+                if s + 1 < STEPS:
+                    soften(s + 1)
+                weigh(s)
+                if s + 2 < STEPS:
+                    values(s + 1)
+                continue
+            if s > 0:
+                soften(s)
+                if s == 1:
+                    quantise(3)
+                if s + QUANTISE_AHEAD < STEPS:
+                    quantise(s + QUANTISE_AHEAD)
             if s + 1 < STEPS:
                 logits(s + 1)
             weigh(s)
+            if s == 0:
+                turn(3, every_bank[2:], (S_COPY,) * 2)
             if s + FETCH_AHEAD < STEPS:
                 fetch(s + FETCH_AHEAD)
             if s + TURN_AHEAD < STEPS:
-                turn(s + TURN_AHEAD, every_bank[: BANKS - 1])
+                turn(s + TURN_AHEAD, every_bank[:3], (S_COPY,) * 3)
             if s > 0:
                 total(s - 1)
             if s + TURN_AHEAD < STEPS:
-                turn(s + TURN_AHEAD, every_bank[BANKS - 1 :])
+                turn(s + TURN_AHEAD, every_bank[3:], (S_COPY,) * 1)
             if s + 1 < STEPS:
                 values(s + 1)
-        for n in range(BATCHES - 1):
-            divide_and_store(n)
+            if s == LATE - 1:
+                logits(s + 2)
+                soften(s + 1)
+        batch = [range(GROUPS * n, GROUPS * (n + 1)) for n in range(BATCHES)]
+        total(STEPS - 2)
         total(STEPS - 1)
-        divide_and_store(BATCHES - 1)
+        root(batch[0])
+        root(batch[1])
+        root(batch[2])
+        root(batch[3][:2])
+        root(batch[3][2:3])
+        root(batch[3][3:])
+        square(batch[2])
+        square(batch[3])
+        times_root(batch[0], True)
+        times_root(batch[1], True)
+        times_root(batch[0], False)
+        store(0)
+        times_root(batch[1], False)
+        store(1)
+        times_root(batch[2], True)
+        store(2)
+        times_root(batch[3][:2], True)
+        times_root(batch[3][2:3], True)
+        times_root(batch[3][3:], True)
+        store(3)

@@ -48,9 +48,8 @@ def tile_tokencompressor_pa_t_kernel(tc, H, W_a_KV, W_b_KV, W_a_Z, W_b_Z, B_a, B
         code_pool = ctx.enter_context(tc.tile_pool(name="codes", bufs=8))
         soft_pool = ctx.enter_context(tc.tile_pool(name="soft", bufs=3))
         out_pool = ctx.enter_context(tc.tile_pool(name="outs", bufs=2))
-        psum_t = ctx.enter_context(tc.psum_pool(name="psum_t", bufs=3))
+        psum_t = ctx.enter_context(tc.psum_pool(name="psum_t", bufs=4))
         psum_mx = ctx.enter_context(tc.psum_pool(name="psum_mx", bufs=1))
-        psum_sum = ctx.enter_context(tc.psum_pool(name="psum_sum", bufs=1))
 
         arrival = [(n, q) for n in range(BATCHES) for q in (3, 0, 1, 2)]
         steps = [(n, q) for n in range(BATCHES) for q in range(GROUPS)]
@@ -290,8 +289,8 @@ def tile_tokencompressor_pa_t_kernel(tc, H, W_a_KV, W_b_KV, W_a_Z, W_b_Z, B_a, B
             halve("weighted", s, weighted)
 
         def total(s):
-            if s < STEPS - 2:
-                sums = psum_sum.tile([P, 2, CHANNELS], F32, tag="sums")
+            if s < LATE - 1:
+                sums = psum_mx.tile([P, 2, CHANNELS], F32, tag="c_b")
             else:
                 sums = psum_t.tile([P, 2, CHANNELS], F32, tag="turned")
             for place, name in enumerate(("weights", "weighted")):
@@ -359,7 +358,7 @@ def tile_tokencompressor_pa_t_kernel(tc, H, W_a_KV, W_b_KV, W_a_Z, W_b_Z, B_a, B
         quantise_weights((W_KV_A, W_KV_B))
         turn(1, pair_banks[0], (S_COPY, S_COPY))
         turn(1, pair_banks[1], (S_COPY, V_COPY))
-        bias_t = psum_sum.tile([P, 2, P], F32, tag="sums")
+        bias_t = psum_mx.tile([P, 2, P], F32, tag="c_b")
         nc.tensor.transpose(bias_t[:, 0, :], bias_rows32[:], ident[:])
         bias = const.tile([P, TERMS], F32)
         nc.scalar.copy(out=bias[:], in_=bias_t[:, 0, 0:TERMS])

@@ -46,7 +46,7 @@ def tile_tokencompressor_pa_t_kernel(tc, H, W_a_KV, W_b_KV, W_a_Z, W_b_Z, B_a, B
         raw_pool = ctx.enter_context(tc.tile_pool(name="raw", bufs=FETCH_AHEAD))
         grouped_pool = ctx.enter_context(tc.tile_pool(name="grouped", bufs=3))
         code_pool = ctx.enter_context(tc.tile_pool(name="codes", bufs=8))
-        soft_pool = ctx.enter_context(tc.tile_pool(name="soft", bufs=3))
+        soft_pool = ctx.enter_context(tc.tile_pool(name="soft", bufs=4))
         out_pool = ctx.enter_context(tc.tile_pool(name="outs", bufs=2))
         psum_t = ctx.enter_context(tc.psum_pool(name="psum_t", bufs=4))
         psum_mx = ctx.enter_context(tc.psum_pool(name="psum_mx", bufs=1))
@@ -304,7 +304,7 @@ def tile_tokencompressor_pa_t_kernel(tc, H, W_a_KV, W_b_KV, W_a_Z, W_b_Z, B_a, B
                         start=(j == 0),
                         stop=(j == terms - 1),
                     )
-            if s < STEPS - 2:
+            if s < STEPS - 3:
                 nc.scalar.copy(out=totals[:, s, :, :], in_=sums[:])
             else:
                 sums_of[s] = sums
@@ -372,22 +372,7 @@ def tile_tokencompressor_pa_t_kernel(tc, H, W_a_KV, W_b_KV, W_a_Z, W_b_Z, B_a, B
         values(0)
         turn(3, every_bank[:2], (S_COPY,) * 2)
         quantise(2)
-        for s in range(STEPS):
-            if s >= LATE:
-                if s < STEPS - 1:
-                    total(s - 1)
-                if s + QUANTISE_AHEAD < STEPS:
-                    quantise(s + QUANTISE_AHEAD)
-                if s + 2 < STEPS:
-                    logits(s + 2)
-                if s + 2 == STEPS:
-                    values(s + 1)
-                if s + 1 < STEPS:
-                    soften(s + 1)
-                weigh(s)
-                if s + 2 < STEPS:
-                    values(s + 1)
-                continue
+        for s in range(LATE):
             if s > 0:
                 soften(s)
                 if s == 1:
@@ -409,18 +394,32 @@ def tile_tokencompressor_pa_t_kernel(tc, H, W_a_KV, W_b_KV, W_a_Z, W_b_Z, B_a, B
                 turn(s + TURN_AHEAD, every_bank[3:], (S_COPY,) * 1)
             if s + 1 < STEPS:
                 values(s + 1)
-            if s == LATE - 1:
-                logits(s + 2)
-                soften(s + 1)
+        logits(LATE + 1)
+        soften(LATE)
+        quantise(STEPS - 1)
+        logits(LATE + 2)
+        total(LATE - 1)
+        soften(LATE + 1)
+        logits(LATE + 3)
+        weigh(LATE)
+        values(LATE + 1)
+        soften(LATE + 2)
+        total(LATE)
+        weigh(LATE + 1)
+        values(LATE + 2)
+        total(LATE + 1)
+        values(LATE + 3)
+        soften(LATE + 3)
+        weigh(LATE + 2)
+        weigh(LATE + 3)
         batch = [range(GROUPS * n, GROUPS * (n + 1)) for n in range(BATCHES)]
         total(STEPS - 2)
         total(STEPS - 1)
         root(batch[0])
         root(batch[1])
         root(batch[2])
-        root(batch[3][:2])
-        root(batch[3][2:3])
-        root(batch[3][3:])
+        for s in batch[3]:
+            root([s])
         square(batch[2])
         square(batch[3])
         times_root(batch[0], True)
@@ -431,7 +430,6 @@ def tile_tokencompressor_pa_t_kernel(tc, H, W_a_KV, W_b_KV, W_a_Z, W_b_Z, B_a, B
         store(1)
         times_root(batch[2], True)
         store(2)
-        times_root(batch[3][:2], True)
-        times_root(batch[3][2:3], True)
-        times_root(batch[3][3:], True)
+        for s in batch[3]:
+            times_root([s], True)
         store(3)

@@ -60,6 +60,7 @@ def tile_tokencompressor_pa_t_kernel(tc, H, W_a_KV, W_b_KV, W_a_Z, W_b_Z, B_a, B
         weights_of = {}
         values_b_of = {}
         sums_of = {}
+        weighted_of = {}
         halved_of = {}
 
         def fetch(i, pieces=1):
@@ -164,42 +165,59 @@ def tile_tokencompressor_pa_t_kernel(tc, H, W_a_KV, W_b_KV, W_a_Z, W_b_Z, B_a, B
             )
             quantised[arrival[i]] = (codes, scales)
 
-        def project(name, w, operand, s, pieces=1):
-            codes, scales = operand
-            if s > LATE and s % 2 == 1 and name in ("z_a", "z_b"):
+        def bank_for(name, s):
+            if s > LATE and s % 2 == 1 and name.startswith("z"):
                 bank = psum_t.tile([P, POSITIONS, ROWS], F32, tag="turned")
             else:
-                tag = name.replace("c_", "z_") if s == STEPS - 1 else name
+                tag = {"c_a": "z_0", "c_b": "z_1"}.get(name, name) if s == STEPS - 1 else name
                 bank = psum_mx.tile([P, POSITIONS, ROWS], F32, tag=tag)
-            sums = bank[:].rearrange("p j r -> p (j r)")
-            width = TOKENS // pieces
-            for piece in range(pieces):
-                mine = slice(width * piece, width * (piece + 1))
-                for g in range(PASSES):
-                    nc.tensor.matmul_mx(
-                        out=sums[:, mine],
-                        lhsT=w_codes[:, PASSES * w + g, :].bitcast(FP8X4),
-                        lhsT_scale=w_scales[:, PASSES * w + g, :],
-                        rhs=codes[:, g, mine].bitcast(FP8X4),
-                        rhs_scale=scales[:, g, mine],
-                        start=(g == 0),
-                        stop=(g == PASSES - 1),
-                    )
-            banks[(name, s)] = bank
+            return bank
+
+        def product(out_, w, operand, columns):
+            codes, scales = operand
+            for g in range(PASSES):
+                nc.tensor.matmul_mx(
+                    out=out_,
+                    lhsT=w_codes[:, PASSES * w + g, :].bitcast(FP8X4),
+                    lhsT_scale=w_scales[:, PASSES * w + g, :],
+                    rhs=codes[:, g, columns].bitcast(FP8X4),
+                    rhs_scale=scales[:, g, columns],
+                    start=(g == 0),
+                    stop=(g == PASSES - 1),
+                )
+
+        def logit_bank(s, pair):
+            if ("z", pair, s) not in banks:
+                bank = bank_for("z_%d" % pair, s)
+                banks[("z", pair, s)] = bank
+            return banks[("z", pair, s)]
+
+        def logits_of(s, side, pair):
+            n, q = steps[s]
+            operand = quantised[(n, (q - side) % GROUPS)]
+            half = TOKENS // PAIRS
+            product(
+                logit_bank(s, pair)[:, 2 * side : 2 * side + 2, :].rearrange("p j r -> p (j r)"),
+                (W_Z_A, W_Z_B)[side],
+                operand,
+                slice(half * pair, half * (pair + 1)),
+            )
 
         def own_and_previous(s):
             n, q = steps[s]
             return quantised[(n, q)], quantised[(n, (q - 1) % GROUPS)]
 
         def logits(s):
-            own, previous = own_and_previous(s)
-            project("z_a", W_Z_A, own, s)
-            project("z_b", W_Z_B, previous, s)
+            for pair in range(PAIRS):
+                for side in range(2):
+                    logits_of(s, side, pair)
 
         def values(s):
             own, previous = own_and_previous(s)
-            project("c_a", W_KV_A, own, s)
-            project("c_b", W_KV_B, previous, s)
+            for name, w, operand in (("c_a", W_KV_A, own), ("c_b", W_KV_B, previous)):
+                bank = bank_for(name, s)
+                product(bank[:].rearrange("p j r -> p (j r)"), w, operand, slice(0, TOKENS))
+                banks[(name, s)] = bank
             if s < STEPS - 1:
                 values_b = soft_pool.tile([P, POSITIONS, ROWS], F32)
                 nc.scalar.copy(out=values_b[:], in_=banks[("c_b", s)][:])
@@ -218,75 +236,85 @@ def tile_tokencompressor_pa_t_kernel(tc, H, W_a_KV, W_b_KV, W_a_Z, W_b_Z, B_a, B
             )
             halved_of[(name, s)] = halved
 
-        def soften(s):
+        def nothing(j):
+            pass
+
+        def soften(s, beside=nothing, behind=lambda: None):
             shift = shift_of(s)
             kept = ROWS - shift
-            z_a = banks[("z_a", s)]
-            z_b = banks[("z_b", s)]
+            z = [banks[("z", pair, s)] for pair in range(PAIRS)]
             top_a = soft_pool.tile([P, ROWS], F32)
             top_b = soft_pool.tile([P, ROWS], F32)
-            nc.vector.tensor_scalar_add(out=top_a[:], in0=z_a[:, 0, :], scalar1=bias[:, 0:1])
+            nc.vector.tensor_scalar_add(out=top_a[:], in0=z[0][:, 0, :], scalar1=bias[:, 0:1])
             nc.vector.tensor_scalar_add(
-                out=top_b[:, shift:], in0=z_b[:, 0, 0:kept], scalar1=bias[:, POSITIONS : POSITIONS + 1]
+                out=top_b[:, shift:], in0=z[0][:, 2, 0:kept], scalar1=bias[:, POSITIONS : POSITIONS + 1]
             )
+            beside(0)
             for j in range(1, POSITIONS):
+                pair, jj = divmod(j, 2)
                 nc.vector.scalar_tensor_tensor(
-                    out=top_a[:], in0=z_a[:, j, :], scalar=bias[:, j : j + 1], in1=top_a[:], op0=ALU.add, op1=ALU.max
+                    out=top_a[:], in0=z[pair][:, jj, :], scalar=bias[:, j : j + 1], in1=top_a[:], op0=ALU.add, op1=ALU.max
                 )
                 nc.vector.scalar_tensor_tensor(
                     out=top_b[:, shift:],
-                    in0=z_b[:, j, 0:kept],
+                    in0=z[pair][:, 2 + jj, 0:kept],
                     scalar=bias[:, POSITIONS + j : POSITIONS + j + 1],
                     in1=top_b[:, shift:],
                     op0=ALU.add,
                     op1=ALU.max,
                 )
+                beside(j)
+            behind()
             nc.vector.tensor_tensor(out=top_a[:, shift:], in0=top_a[:, shift:], in1=top_b[:, shift:], op=ALU.max)
 
             weights = soft_pool.tile([P, TERMS, ROWS], F32)
-            for j in range(POSITIONS):
-                nc.vector.scalar_tensor_tensor(
-                    out=weights[:, j, :],
-                    in0=z_a[:, j, :],
-                    scalar=bias[:, j : j + 1],
-                    in1=top_a[:],
-                    op0=ALU.add,
-                    op1=ALU.subtract,
-                )
-            nc.scalar.activation(out=weights[:, 0:POSITIONS, :], in_=weights[:, 0:POSITIONS, :], func=ACT.Exp)
             if shift:
                 nc.vector.memset(weights[:, POSITIONS:TERMS, 0:shift], NEG)
-            for j in range(POSITIONS):
-                nc.vector.scalar_tensor_tensor(
-                    out=weights[:, POSITIONS + j, shift:],
-                    in0=z_b[:, j, 0:kept],
-                    scalar=bias[:, POSITIONS + j : POSITIONS + j + 1],
-                    in1=top_a[:, shift:],
-                    op0=ALU.add,
-                    op1=ALU.subtract,
-                )
-            nc.scalar.activation(out=weights[:, POSITIONS:TERMS, :], in_=weights[:, POSITIONS:TERMS, :], func=ACT.Exp)
+            for pair in range(PAIRS):
+                for side in range(2):
+                    for jj in range(2):
+                        term = POSITIONS * side + 2 * pair + jj
+                        start, width = (shift, kept) if side else (0, ROWS)
+                        nc.vector.scalar_tensor_tensor(
+                            out=weights[:, term, start:],
+                            in0=z[pair][:, 2 * side + jj, 0:width],
+                            scalar=bias[:, term : term + 1],
+                            in1=top_a[:, start:],
+                            op0=ALU.add,
+                            op1=ALU.subtract,
+                        )
+            for side in range(2):
+                mine = weights[:, POSITIONS * side : POSITIONS * (side + 1), :]
+                nc.scalar.activation(out=mine, in_=mine, func=ACT.Exp)
             weights_of[s] = weights
             halve("weights", s, weights)
 
-        def weigh(s):
+        def weigh_b(s):
             shift = shift_of(s)
-            kept = ROWS - shift
-            weights = weights_of[s]
             weighted = soft_pool.tile([P, TERMS, ROWS], F32)
-            nc.vector.tensor_tensor(
-                out=weighted[:, 0:POSITIONS, :], in0=banks[("c_a", s)][:], in1=weights[:, 0:POSITIONS, :], op=ALU.mult
-            )
+            weighted_of[s] = weighted
             if shift:
                 nc.gpsimd.memset(weighted[:, POSITIONS:TERMS, 0:shift], 0.0)
             engine, values_b = (nc.gpsimd, values_b_of[s]) if s < STEPS - 1 else (nc.vector, banks[("c_b", s)])
             engine.tensor_tensor(
                 out=weighted[:, POSITIONS:TERMS, shift:],
-                in0=values_b[:, :, 0:kept],
-                in1=weights[:, POSITIONS:TERMS, shift:],
+                in0=values_b[:, :, 0 : ROWS - shift],
+                in1=weights_of[s][:, POSITIONS:TERMS, shift:],
                 op=ALU.mult,
             )
-            halve("weighted", s, weighted)
+
+        def weigh_a(s, terms):
+            nc.vector.tensor_tensor(
+                out=weighted_of[s][:, terms, :],
+                in0=banks[("c_a", s)][:, terms, :],
+                in1=weights_of[s][:, terms, :],
+                op=ALU.mult,
+            )
+
+        def weigh(s):
+            weigh_b(s)
+            weigh_a(s, slice(0, POSITIONS))
+            halve("weighted", s, weighted_of[s])
 
         def total(s):
             if s < LATE - 1:
@@ -362,40 +390,43 @@ def tile_tokencompressor_pa_t_kernel(tc, H, W_a_KV, W_b_KV, W_a_Z, W_b_Z, B_a, B
         nc.tensor.transpose(bias_t[:, 0, :], bias_rows32[:], ident[:])
         bias = const.tile([P, TERMS], F32)
         nc.scalar.copy(out=bias[:], in_=bias_t[:, 0, 0:TERMS])
-        project("z_b", W_Z_B, quantised[arrival[0]], 0)
+        for pair in range(PAIRS):
+            logits_of(0, 1, pair)
         quantise_pair(1, 0)
         quantise_pair(1, 1)
-        project("z_a", W_Z_A, quantised[arrival[1]], 0, PAIRS)
+        for pair in range(PAIRS):
+            logits_of(0, 0, pair)
         turn(2, every_bank[:3], (S_COPY,) * 3)
         soften(0)
         turn(2, every_bank[3:], (V_COPY,))
         values(0)
         turn(3, every_bank[:2], (S_COPY,) * 2)
         quantise(2)
+        def soften_and_weigh(s):
+            def behind():
+                halve("weighted", s - 1, weighted_of[s - 1])
+                values(s)
+
+            soften(s, lambda j: weigh_a(s - 1, slice(j, j + 1)), behind)
+
         for s in range(LATE):
             if s > 0:
-                soften(s)
+                soften_and_weigh(s)
                 if s == 1:
                     quantise(3)
-                if s + QUANTISE_AHEAD < STEPS:
-                    quantise(s + QUANTISE_AHEAD)
-            if s + 1 < STEPS:
-                logits(s + 1)
-            weigh(s)
+                quantise(s + QUANTISE_AHEAD)
+            logits(s + 1)
+            weigh_b(s)
             if s == 0:
                 turn(3, every_bank[2:], (S_COPY,) * 2)
             if s + FETCH_AHEAD < STEPS:
                 fetch(s + FETCH_AHEAD)
-            if s + TURN_AHEAD < STEPS:
-                turn(s + TURN_AHEAD, every_bank[:3], (S_COPY,) * 3)
+            turn(s + TURN_AHEAD, every_bank[:3], (S_COPY,) * 3)
             if s > 0:
                 total(s - 1)
-            if s + TURN_AHEAD < STEPS:
-                turn(s + TURN_AHEAD, every_bank[3:], (S_COPY,) * 1)
-            if s + 1 < STEPS:
-                values(s + 1)
+            turn(s + TURN_AHEAD, every_bank[3:], (S_COPY,) * 1)
         logits(LATE + 1)
-        soften(LATE)
+        soften_and_weigh(LATE)
         quantise(STEPS - 1)
         logits(LATE + 2)
         total(LATE - 1)

from contextlib import ExitStack

import concourse.mybir as mybir
from concourse.masks import make_identity

F32 = mybir.dt.float32
BF16 = mybir.dt.bfloat16
U32 = mybir.dt.uint32
U8 = mybir.dt.uint8
FP8X4 = mybir.dt.float8_e4m3fn_x4
ALU = mybir.AluOpType
ACT = mybir.ActivationFunctionType

P = 128
BATCHES = 4
FEATURES = 1024
CHANNELS = 128
POSITIONS = 4
GROUPS = 4
ROWS = 128
PASSES = 2
HALVES = 2
VALUES = 4
TOKENS = POSITIONS * ROWS
WORDS = FEATURES // 2
TERMS = 2 * POSITIONS
NEG = -1e30
W_KV_A, W_KV_B, W_Z_A, W_Z_B = 0, 1, 2, 3
STEPS = BATCHES * GROUPS
QUANTISE_AHEAD = 3
TURN_AHEAD = 4
FETCH_AHEAD = 6
HEAD = 2
PAIRS = 2
LATE = STEPS - TURN_AHEAD
BANKS = PASSES * POSITIONS // 2

FLOPS = 2 * BATCHES * GROUPS * TOKENS * FEATURES * 4 * CHANNELS


def tile_tokencompressor_pa_t_kernel(tc, H, W_a_KV, W_b_KV, W_a_Z, W_b_Z, B_a, B_b, out):
    nc = tc.nc
    with ExitStack() as ctx:
        ctx.enter_context(tc.manual_schedule())
        const = ctx.enter_context(tc.tile_pool(name="const", bufs=1))
        raw_pool = ctx.enter_context(tc.tile_pool(name="raw", bufs=FETCH_AHEAD))
        grouped_pool = ctx.enter_context(tc.tile_pool(name="grouped", bufs=3))
        code_pool = ctx.enter_context(tc.tile_pool(name="codes", bufs=8))
        soft_pool = ctx.enter_context(tc.tile_pool(name="soft", bufs=4))
        out_pool = ctx.enter_context(tc.tile_pool(name="outs", bufs=2))
        psum_t = ctx.enter_context(tc.psum_pool(name="psum_t", bufs=4))
        psum_mx = ctx.enter_context(tc.psum_pool(name="psum_mx", bufs=1))

        arrival = [(n, q) for n in range(BATCHES) for q in (3, 0, 1, 2)]
        steps = [(n, q) for n in range(BATCHES) for q in range(GROUPS)]
        raw_of = {}
        grouped_of = {}
        quantised = {}
        banks = {}
        weights_of = {}
        values_b_of = {}
        sums_of = {}
        weighted_of = {}
        halved_of = {}

        def fetch(i, pieces=1):
            n, q = arrival[i]
            raw = raw_pool.tile([P, POSITIONS, FEATURES], BF16)
            rows = H[n].rearrange("(r q j) k -> q r j k", q=GROUPS, j=POSITIONS)[q]
            for piece in range(pieces):
                mine = slice(piece * POSITIONS // pieces, (piece + 1) * POSITIONS // pieces)
                nc.sync.dma_start(out=raw[:, mine, :], in_=rows[:, mine, :])
            raw_of[i] = raw

        w_raw = const.tile([P, 4, PASSES, VALUES * CHANNELS], BF16)
        weights_in = (W_a_KV, W_b_KV, W_a_Z, W_b_Z)

        def fetch_weights(places):
            for w in places:
                nc.sync.dma_start(
                    out=w_raw[:, w, :, :], in_=weights_in[w].rearrange("(g p t) c -> p g (t c)", g=PASSES, t=VALUES)
                )

        bias_rows = const.tile([P, CHANNELS], BF16)
        nc.vector.memset(bias_rows[:], 0.0)
        fetch_weights((W_Z_A, W_Z_B))
        nc.sync.dma_start(out=bias_rows[0:POSITIONS, :], in_=B_a)
        nc.sync.dma_start(out=bias_rows[POSITIONS:TERMS, :], in_=B_b)
        fetch(0, PAIRS)
        fetch_weights((W_KV_A, W_KV_B))
        fetch(1, PAIRS)
        for i in range(HEAD, FETCH_AHEAD):
            fetch(i)

        ident = const.tile([P, P], F32)
        make_identity(nc, ident[:])

        bias_rows32 = const.tile([P, CHANNELS], F32)
        nc.gpsimd.tensor_copy(out=bias_rows32[:], in_=bias_rows[:])

        w_grouped = const.tile([P, 4 * PASSES, CHANNELS, VALUES], BF16, align_bytes=64)
        w_codes = const.tile([P, 4 * PASSES, CHANNELS], U32, align_bytes=64)
        w_scales = const.tile([P, 4 * PASSES, CHANNELS], U8, align_bytes=64)

        def group_weights(places):
            for w in places:
                nc.vector.tensor_copy(
                    out=w_grouped[:, PASSES * w : PASSES * (w + 1), :, :],
                    in_=w_raw[:, w, :, :].rearrange("p g (t c) -> p g c t", t=VALUES),
                )

        def quantise_weights(places):
            mine = slice(PASSES * places[0], PASSES * (places[-1] + 1))
            nc.vector.quantize_mx(
                out=w_codes[:, mine, :].rearrange("p a c -> p (a c)").bitcast(FP8X4),
                scales=w_scales[:, mine, :].rearrange("p a c -> p (a c)"),
                in_=w_grouped[:, mine, :, :].rearrange("p a c t -> p (a c t)"),
            )

        totals = const.tile([P, STEPS, 2, CHANNELS], F32)

        def turn(i, some_banks, copies):
            raw_words = raw_of[i][:].bitcast(F32)
            if i not in grouped_of:
                grouped = grouped_pool.tile([P, PASSES, 4 * TOKENS], BF16, align_bytes=64)
                grouped_of[i] = grouped
            for bank, copy in zip(some_banks, copies):
                g, pair = divmod(bank, POSITIONS // 2)
                turned = psum_t.tile([P, HALVES, 2, ROWS], F32, tag="turned")
                for u in range(HALVES):
                    for jj in range(2):
                        nc.tensor.transpose(
                            turned[:, u, jj, :],
                            raw_words[:, 2 * pair + jj, 2 * P * g + u : 2 * P * (g + 1) : HALVES],
                            ident[:],
                        )
                columns = grouped_of[i][:, g, 8 * ROWS * pair : 8 * ROWS * (pair + 1)].bitcast(F32)
                copy(
                    out=columns.rearrange("p (c u) -> p c u", u=HALVES),
                    in_=turned[:].rearrange("p u j r -> p (j r) u"),
                )

        def quantise_pair(i, pair):
            if arrival[i] not in quantised:
                codes = code_pool.tile([P, PASSES, TOKENS], U32, tag="codes", align_bytes=64)
                scales = code_pool.tile([P, PASSES, TOKENS], U8, tag="scales", align_bytes=64)
                quantised[arrival[i]] = (codes, scales)
            codes, scales = quantised[arrival[i]]
            width = TOKENS // PAIRS
            for g in range(PASSES):
                mine = slice(width * pair, width * (pair + 1))
                nc.vector.quantize_mx(
                    out=codes[:, g, mine].bitcast(FP8X4),
                    scales=scales[:, g, mine],
                    in_=grouped_of[i][:, g, VALUES * width * pair : VALUES * width * (pair + 1)],
                )

        def quantise(i):
            codes = code_pool.tile([P, PASSES, TOKENS], U32, tag="codes", align_bytes=64)
            scales = code_pool.tile([P, PASSES, TOKENS], U8, tag="scales", align_bytes=64)
            nc.vector.quantize_mx(
                out=codes[:].rearrange("p g c -> p (g c)").bitcast(FP8X4),
                scales=scales[:].rearrange("p g c -> p (g c)"),
                in_=grouped_of[i][:].rearrange("p g c -> p (g c)"),
            )
            quantised[arrival[i]] = (codes, scales)

        def bank_for(name, s):
            if s > LATE and s % 2 == 1 and name.startswith("z"):
                bank = psum_t.tile([P, POSITIONS, ROWS], F32, tag="turned")
            else:
                tag = {"c_a": "z_0", "c_b": "z_1"}.get(name, name) if s == STEPS - 1 else name
                bank = psum_mx.tile([P, POSITIONS, ROWS], F32, tag=tag)
            return bank

        def product(out_, w, operand, columns):
            codes, scales = operand
            for g in range(PASSES):
                nc.tensor.matmul_mx(
                    out=out_,
                    lhsT=w_codes[:, PASSES * w + g, :].bitcast(FP8X4),
                    lhsT_scale=w_scales[:, PASSES * w + g, :],
                    rhs=codes[:, g, columns].bitcast(FP8X4),
                    rhs_scale=scales[:, g, columns],
                    start=(g == 0),
                    stop=(g == PASSES - 1),
                )

        def logit_bank(s, pair):
            if ("z", pair, s) not in banks:
                bank = bank_for("z_%d" % pair, s)
                banks[("z", pair, s)] = bank
            return banks[("z", pair, s)]

        def logits_of(s, side, pair):
            n, q = steps[s]
            operand = quantised[(n, (q - side) % GROUPS)]
            half = TOKENS // PAIRS
            product(
                logit_bank(s, pair)[:, 2 * side : 2 * side + 2, :].rearrange("p j r -> p (j r)"),
                (W_Z_A, W_Z_B)[side],
                operand,
                slice(half * pair, half * (pair + 1)),
            )

        def own_and_previous(s):
            n, q = steps[s]
            return quantised[(n, q)], quantised[(n, (q - 1) % GROUPS)]

        def logits(s):
            for pair in range(PAIRS):
                for side in range(2):
                    logits_of(s, side, pair)

        def values(s):
            own, previous = own_and_previous(s)
            for name, w, operand in (("c_a", W_KV_A, own), ("c_b", W_KV_B, previous)):
                bank = bank_for(name, s)
                product(bank[:].rearrange("p j r -> p (j r)"), w, operand, slice(0, TOKENS))
                banks[(name, s)] = bank
            if s < STEPS - 1:
                values_b = soft_pool.tile([P, POSITIONS, ROWS], F32)
                nc.scalar.copy(out=values_b[:], in_=banks[("c_b", s)][:])
                values_b_of[s] = values_b

        def shift_of(s):
            return 1 if steps[s][1] == 0 else 0

        def halve(name, s, terms):
            if s >= LATE:
                halved_of[(name, s)] = terms
                return
            halved = soft_pool.tile([P, POSITIONS, ROWS], F32, tag=name + "_halved")
            nc.gpsimd.tensor_tensor(
                out=halved[:], in0=terms[:, 0:POSITIONS, :], in1=terms[:, POSITIONS:TERMS, :], op=ALU.add
            )
            halved_of[(name, s)] = halved

        def nothing(j):
            pass

        def soften(s, beside=nothing, behind=lambda: None):
            shift = shift_of(s)
            kept = ROWS - shift
            z = [banks[("z", pair, s)] for pair in range(PAIRS)]
            top_a = soft_pool.tile([P, ROWS], F32)
            top_b = soft_pool.tile([P, ROWS], F32)
            nc.vector.tensor_scalar_add(out=top_a[:], in0=z[0][:, 0, :], scalar1=bias[:, 0:1])
            nc.vector.tensor_scalar_add(
                out=top_b[:, shift:], in0=z[0][:, 2, 0:kept], scalar1=bias[:, POSITIONS : POSITIONS + 1]
            )
            beside(0)
            for j in range(1, POSITIONS):
                pair, jj = divmod(j, 2)
                nc.vector.scalar_tensor_tensor(
                    out=top_a[:], in0=z[pair][:, jj, :], scalar=bias[:, j : j + 1], in1=top_a[:], op0=ALU.add, op1=ALU.max
                )
                nc.vector.scalar_tensor_tensor(
                    out=top_b[:, shift:],
                    in0=z[pair][:, 2 + jj, 0:kept],
                    scalar=bias[:, POSITIONS + j : POSITIONS + j + 1],
                    in1=top_b[:, shift:],
                    op0=ALU.add,
                    op1=ALU.max,
                )
                beside(j)
            behind()
            nc.vector.tensor_tensor(out=top_a[:, shift:], in0=top_a[:, shift:], in1=top_b[:, shift:], op=ALU.max)

            weights = soft_pool.tile([P, TERMS, ROWS], F32)
            if shift:
                nc.vector.memset(weights[:, POSITIONS:TERMS, 0:shift], NEG)
            for pair in range(PAIRS):
                for side in range(2):
                    for jj in range(2):
                        term = POSITIONS * side + 2 * pair + jj
                        start, width = (shift, kept) if side else (0, ROWS)
                        nc.vector.scalar_tensor_tensor(
                            out=weights[:, term, start:],
                            in0=z[pair][:, 2 * side + jj, 0:width],
                            scalar=bias[:, term : term + 1],
                            in1=top_a[:, start:],
                            op0=ALU.add,
                            op1=ALU.subtract,
                        )
            for side in range(2):
                mine = weights[:, POSITIONS * side : POSITIONS * (side + 1), :]
                nc.scalar.activation(out=mine, in_=mine, func=ACT.Exp)
            weights_of[s] = weights
            halve("weights", s, weights)

        def weigh_b(s):
            shift = shift_of(s)
            weighted = soft_pool.tile([P, TERMS, ROWS], F32)
            weighted_of[s] = weighted
            if shift:
                nc.gpsimd.memset(weighted[:, POSITIONS:TERMS, 0:shift], 0.0)
            engine, values_b = (nc.gpsimd, values_b_of[s]) if s < STEPS - 1 else (nc.vector, banks[("c_b", s)])
            engine.tensor_tensor(
                out=weighted[:, POSITIONS:TERMS, shift:],
                in0=values_b[:, :, 0 : ROWS - shift],
                in1=weights_of[s][:, POSITIONS:TERMS, shift:],
                op=ALU.mult,
            )

        def weigh_a(s, terms):
            nc.vector.tensor_tensor(
                out=weighted_of[s][:, terms, :],
                in0=banks[("c_a", s)][:, terms, :],
                in1=weights_of[s][:, terms, :],
                op=ALU.mult,
            )

        def weigh(s):
            weigh_b(s)
            weigh_a(s, slice(0, POSITIONS))
            halve("weighted", s, weighted_of[s])

        def total(s):
            if s < LATE - 1:
                sums = psum_mx.tile([P, 2, CHANNELS], F32, tag="c_b")
            else:
                sums = psum_t.tile([P, 2, CHANNELS], F32, tag="turned")
            for place, name in enumerate(("weights", "weighted")):
                terms = POSITIONS if s < LATE else TERMS
                for j in range(terms):
                    nc.tensor.matmul(
                        out=sums[:, place, :],
                        lhsT=halved_of[(name, s)][:, j, :],
                        rhs=ident[:],
                        is_transpose=True,
                        start=(j == 0),
                        stop=(j == terms - 1),
                    )
            if s < STEPS - 3:
                nc.scalar.copy(out=totals[:, s, :, :], in_=sums[:])
            else:
                sums_of[s] = sums

        roots = const.tile([P, STEPS, CHANNELS], F32)
        results = const.tile([P, STEPS, CHANNELS], F32)

        def steps_of(part):
            return slice(part[0], part[-1] + 1)

        def both_sums(part, place):
            if part[0] in sums_of:
                return sums_of[part[0]][:, place, :]
            return totals[:, steps_of(part), place, :]

        def root(part):
            out_ = roots[:, part[0], :] if part[0] in sums_of else roots[:, steps_of(part), :]
            nc.scalar.activation(out=out_, in_=both_sums(part, 0), func=ACT.Abs_reciprocal_sqrt)

        def square(part):
            mine = roots[:, steps_of(part), :]
            nc.scalar.activation(out=mine, in_=mine, func=ACT.Square)

        def times_root(part, first):
            one = part[0] in sums_of
            mine = results[:, part[0], :] if one else results[:, steps_of(part), :]
            nc.vector.tensor_tensor(
                out=mine,
                in0=both_sums(part, 1) if first else mine,
                in1=roots[:, part[0], :] if one else roots[:, steps_of(part), :],
                op=ALU.mult,
            )

        def store(n):
            mine = slice(GROUPS * n, GROUPS * (n + 1))
            nc.sync.dma_start(
                out=out[n].rearrange("(r q) c -> r (q c)", q=GROUPS), in_=results[:, mine, :].rearrange("r q c -> r (q c)")
            )

        S_COPY, V_COPY = nc.scalar.copy, nc.vector.tensor_copy
        every_bank = range(BANKS)
        pair_banks = [[g * PAIRS + pair for g in range(PASSES)] for pair in range(PAIRS)]

        group_weights((W_Z_A, W_Z_B))
        quantise_weights((W_Z_A, W_Z_B))
        turn(0, pair_banks[0], (S_COPY, S_COPY))
        turn(0, pair_banks[1], (S_COPY, S_COPY))
        quantise_pair(0, 0)
        group_weights((W_KV_A, W_KV_B))
        quantise_pair(0, 1)
        quantise_weights((W_KV_A, W_KV_B))
        turn(1, pair_banks[0], (S_COPY, S_COPY))
        turn(1, pair_banks[1], (S_COPY, V_COPY))
        bias_t = psum_mx.tile([P, 2, P], F32, tag="c_b")
        nc.tensor.transpose(bias_t[:, 0, :], bias_rows32[:], ident[:])
        bias = const.tile([P, TERMS], F32)
        nc.scalar.copy(out=bias[:], in_=bias_t[:, 0, 0:TERMS])
        for pair in range(PAIRS):
            logits_of(0, 1, pair)
        quantise_pair(1, 0)
        quantise_pair(1, 1)
        for pair in range(PAIRS):
            logits_of(0, 0, pair)
        turn(2, every_bank[:3], (S_COPY,) * 3)
        soften(0)
        turn(2, every_bank[3:], (V_COPY,))
        values(0)
        turn(3, every_bank[:2], (S_COPY,) * 2)
        quantise(2)
        def soften_and_weigh(s):
            def behind():
                halve("weighted", s - 1, weighted_of[s - 1])
                values(s)

            soften(s, lambda j: weigh_a(s - 1, slice(j, j + 1)), behind)

        for s in range(LATE):
            if s > 0:
                soften_and_weigh(s)
                if s == 1:
                    quantise(3)
                quantise(s + QUANTISE_AHEAD)
            logits(s + 1)
            weigh_b(s)
            if s == 0:
                turn(3, every_bank[2:], (S_COPY,) * 2)
            if s + FETCH_AHEAD < STEPS:
                fetch(s + FETCH_AHEAD)
            turn(s + TURN_AHEAD, every_bank[:3], (S_COPY,) * 3)
            if s > 0:
                total(s - 1)
            turn(s + TURN_AHEAD, every_bank[3:], (S_COPY,) * 1)
        logits(LATE + 1)
        soften_and_weigh(LATE)
        quantise(STEPS - 1)
        logits(LATE + 2)
        total(LATE - 1)
        soften(LATE + 1)
        logits(LATE + 3)
        weigh(LATE)
        values(LATE + 1)
        soften(LATE + 2)
        total(LATE)
        weigh(LATE + 1)
        values(LATE + 2)
        total(LATE + 1)
        values(LATE + 3)
        soften(LATE + 3)
        weigh(LATE + 2)
        weigh(LATE + 3)
        batch = [range(GROUPS * n, GROUPS * (n + 1)) for n in range(BATCHES)]
        total(STEPS - 2)
        total(STEPS - 1)
        root(batch[0])
        root(batch[1])
        root(batch[2])
        for s in batch[3]:
            root([s])
        square(batch[2])
        square(batch[3])
        times_root(batch[0], True)
        times_root(batch[1], True)
        times_root(batch[0], False)
        store(0)
        times_root(batch[1], False)
        store(1)
        times_root(batch[2], True)
        store(2)
        for s in batch[3]:
            times_root([s], True)
        store(3)
